import numpy as np
import ml_dtypes

BF16 = ml_dtypes.bfloat16


def bf(x):
    return np.asarray(x, np.float32).astype(BF16)


def f32(x):
    return np.asarray(x, np.float32)


def f64(x):
    return np.asarray(x).astype(np.float64)


def striped(idx):
    return np.tile(idx.reshape(-1, 16).T, (8, 1))


C, S, M, N, R = 128, 2048, 256, 512, 4
SCALING = 1.0 / R


def sigmoid(v):
    return 1.0 / (1.0 + np.exp(-v))


def setup_inputs():
    return {"skill_logits": f32(2.0 * np.random.standard_normal((C, S))), "a_w": bf(8.0 * np.random.standard_normal((C, M))), "offs": striped(np.random.permutation(np.tile(np.arange(S), 2))[:N])}


def reference(skill_logits, a_w, offs):
    idx = offs[:16].T.reshape(-1)
    s = sigmoid(f64(skill_logits)[:, idx])
    p = s / s.sum(axis=0, keepdims=True)
    return SCALING * (f64(a_w).T @ p)

@@ -1,0 +1,53 @@
+import concourse.mybir as mybir
+
+F32 = mybir.dt.float32
+BF16 = mybir.dt.bfloat16
+U16 = mybir.dt.uint16
+COPY = mybir.ActivationFunctionType.Copy
+SIGMOID = mybir.ActivationFunctionType.Sigmoid
+MULT = mybir.AluOpType.mult
+
+SKILLS = 128
+TASKS = 2048
+ENTRIES = 256
+SAMPLES = 512
+SCALING = 0.25
+
+FLOPS = 2 * SKILLS * ENTRIES * SAMPLES
+BYTES = 4 * SKILLS * SAMPLES + 2 * SKILLS * ENTRIES + 2 * SKILLS * (SAMPLES // 16) + 4 * ENTRIES * SAMPLES
+
+
+def tile_skilledloralinear_kernel(tc, skill_logits, a_w, offs, out):
+    nc = tc.nc
+    with (
+        tc.tile_pool(name="held", bufs=1) as held,
+        tc.psum_pool(name="psum", bufs=1) as psum,
+    ):
+        offsets = held.tile([SKILLS, SAMPLES // 16], U16, name="offsets")
+        nc.sync.dma_start(offsets[:], offs)
+        logits = held.tile([SKILLS, TASKS], F32, name="logits")
+        nc.sync.dma_start(logits[:], skill_logits)
+        weights = held.tile([SKILLS, ENTRIES], BF16, name="weights")
+        nc.scalar.dma_start(weights[:], a_w)
+
+        ones = held.tile([SKILLS, SKILLS], BF16, name="ones")
+        nc.vector.memset(ones[:], 1.0)
+
+        picked = held.tile([SKILLS, SAMPLES], F32, name="picked")
+        nc.scalar.activation(picked[:], logits[:].indirect(offsets[:]), COPY)
+
+        s = held.tile([SKILLS, SAMPLES], BF16, name="s")
+        nc.scalar.activation(s[:], picked[:], SIGMOID)
+
+        total = psum.tile([SKILLS, SAMPLES], F32, name="total")
+        nc.tensor.matmul(total[:], ones[:], s[:], start=True, stop=True)
+        inverse = held.tile([SKILLS, SAMPLES], F32, name="inverse")
+        nc.vector.reciprocal(inverse[:], total[:])
+
+        for block in range(ENTRIES // 128):
+            rows = slice(block * 128, (block + 1) * 128)
+            mixed = psum.tile([128, SAMPLES], F32, name=f"mixed{block}")
+            nc.tensor.matmul(mixed[:], weights[:, rows], s[:], start=True, stop=True)
+            result = held.tile([128, SAMPLES], F32, name=f"result{block}")
+            nc.vector.scalar_tensor_tensor(result[:], mixed[:], SCALING, inverse[:], MULT, MULT)
+            nc.sync.dma_start(out[rows, :], result[:])

@@ -33,6 +33,10 @@ def tile_skilledloralinear_kernel(tc, skill_logits, a_w, offs, out):
         ones = held.tile([SKILLS, SKILLS], BF16, name="ones")
         nc.vector.memset(ones[:], 1.0)
 
+        scratch = held.tile([SKILLS, 1], F32, name="scratch")
+        nc.vector.memset(scratch[:], 0.0)
+        nc.scalar.activation(scratch[:], scratch[:], SIGMOID)
+
         picked = held.tile([SKILLS, SAMPLES], F32, name="picked")
         nc.scalar.activation(picked[:], logits[:].indirect(offsets[:]), COPY)
 

@@ -1,3 +1,4 @@
+import concourse.masks as masks
 import concourse.mybir as mybir
 
 F32 = mybir.dt.float32
@@ -7,6 +8,7 @@ COPY = mybir.ActivationFunctionType.Copy
 SIGMOID = mybir.ActivationFunctionType.Sigmoid
 MULT = mybir.AluOpType.mult
 
+P = 128
 SKILLS = 128
 TASKS = 2048
 ENTRIES = 256
@@ -30,8 +32,10 @@ def tile_skilledloralinear_kernel(tc, skill_logits, a_w, offs, out):
         weights = held.tile([SKILLS, ENTRIES], BF16, name="weights")
         nc.scalar.dma_start(weights[:], a_w)
 
-        ones = held.tile([SKILLS, SKILLS], BF16, name="ones")
-        nc.vector.memset(ones[:], 1.0)
+        ones_column = held.tile([SKILLS, 1], BF16, name="ones_column")
+        nc.vector.memset(ones_column[:], 1.0)
+        identity = held.tile([P, P], F32, name="identity")
+        masks.make_identity(nc, identity[:])
 
         scratch = held.tile([SKILLS, 1], F32, name="scratch")
         nc.vector.memset(scratch[:], 0.0)
@@ -43,15 +47,25 @@ def tile_skilledloralinear_kernel(tc, skill_logits, a_w, offs, out):
         s = held.tile([SKILLS, SAMPLES], BF16, name="s")
         nc.scalar.activation(s[:], picked[:], SIGMOID)
 
-        total = psum.tile([SKILLS, SAMPLES], F32, name="total")
-        nc.tensor.matmul(total[:], ones[:], s[:], start=True, stop=True)
-        inverse = held.tile([SKILLS, SAMPLES], F32, name="inverse")
-        nc.vector.reciprocal(inverse[:], total[:])
+        totals = psum.tile([P, SAMPLES // P], F32, name="totals")
+        for b in range(SAMPLES // P):
+            nc.tensor.matmul(totals[:, b : b + 1], s[:, b * P : (b + 1) * P], ones_column[:], start=True, stop=True)
+        inverse = held.tile([P, SAMPLES // P], F32, name="inverse")
+        nc.vector.reciprocal(inverse[:], totals[:])
 
-        for block in range(ENTRIES // 128):
-            rows = slice(block * 128, (block + 1) * 128)
-            mixed = psum.tile([128, SAMPLES], F32, name=f"mixed{block}")
-            nc.tensor.matmul(mixed[:], weights[:, rows], s[:], start=True, stop=True)
-            result = held.tile([128, SAMPLES], F32, name=f"result{block}")
-            nc.vector.scalar_tensor_tensor(result[:], mixed[:], SCALING, inverse[:], MULT, MULT)
-            nc.sync.dma_start(out[rows, :], result[:])
+        mixed = []
+        for block in range(ENTRIES // P):
+            product = psum.tile([P, SAMPLES], F32, name=f"product{block}")
+            nc.tensor.matmul(product[:], weights[:, block * P : (block + 1) * P], s[:], start=True, stop=True)
+            scaled = held.tile([P, SAMPLES], F32, name=f"scaled{block}")
+            nc.scalar.mul(scaled[:], product[:], SCALING)
+            mixed.append(scaled)
+
+        spread = psum.tile([P, SAMPLES], F32, name="spread")
+        for b in range(SAMPLES // P):
+            nc.tensor.transpose(spread[:, b * P : (b + 1) * P], inverse[:, b : b + 1].to_broadcast([P, P]), identity[:])
+
+        for block in range(ENTRIES // P):
+            result = held.tile([P, SAMPLES], F32, name=f"result{block}")
+            nc.vector.tensor_tensor(result[:], mixed[block][:], spread[:], MULT)
+            nc.sync.dma_start(out[block * P : (block + 1) * P, :], result[:])

@@ -13,6 +13,7 @@ SKILLS = 128
 TASKS = 2048
 ENTRIES = 256
 SAMPLES = 512
+PIECE = 256
 SCALING = 0.25
 
 FLOPS = 2 * SKILLS * ENTRIES * SAMPLES
@@ -41,31 +42,37 @@ def tile_skilledloralinear_kernel(tc, skill_logits, a_w, offs, out):
         nc.vector.memset(scratch[:], 0.0)
         nc.scalar.activation(scratch[:], scratch[:], SIGMOID)
 
-        picked = held.tile([SKILLS, SAMPLES], F32, name="picked")
-        nc.scalar.activation(picked[:], logits[:].indirect(offsets[:]), COPY)
+        routing = []
+        for piece in range(SAMPLES // PIECE):
+            picked = held.tile([SKILLS, PIECE], F32, name=f"picked{piece}")
+            piece_offsets = offsets[:, piece * (PIECE // 16) : (piece + 1) * (PIECE // 16)]
+            nc.scalar.activation(picked[:], logits[:].indirect(piece_offsets), COPY)
+            s = held.tile([SKILLS, PIECE], BF16, name=f"s{piece}")
+            nc.scalar.activation(s[:], picked[:], SIGMOID)
+            routing.append(s)
 
-        s = held.tile([SKILLS, SAMPLES], BF16, name="s")
-        nc.scalar.activation(s[:], picked[:], SIGMOID)
+        for piece in range(SAMPLES // PIECE):
+            s = routing[piece]
 
-        totals = psum.tile([P, SAMPLES // P], F32, name="totals")
-        for b in range(SAMPLES // P):
-            nc.tensor.matmul(totals[:, b : b + 1], s[:, b * P : (b + 1) * P], ones_column[:], start=True, stop=True)
-        inverse = held.tile([P, SAMPLES // P], F32, name="inverse")
-        nc.vector.reciprocal(inverse[:], totals[:])
+            totals = psum.tile([P, PIECE // P], F32, name=f"totals{piece}")
+            for b in range(PIECE // P):
+                nc.tensor.matmul(totals[:, b : b + 1], s[:, b * P : (b + 1) * P], ones_column[:], start=True, stop=True)
+            inverse = held.tile([P, PIECE // P], F32, name=f"inverse{piece}")
+            nc.vector.reciprocal(inverse[:], totals[:])
 
-        mixed = []
-        for block in range(ENTRIES // P):
-            product = psum.tile([P, SAMPLES], F32, name=f"product{block}")
-            nc.tensor.matmul(product[:], weights[:, block * P : (block + 1) * P], s[:], start=True, stop=True)
-            scaled = held.tile([P, SAMPLES], F32, name=f"scaled{block}")
-            nc.scalar.mul(scaled[:], product[:], SCALING)
-            mixed.append(scaled)
+            mixed = []
+            for block in range(ENTRIES // P):
+                product = psum.tile([P, PIECE], F32, name=f"product{piece}{block}")
+                nc.tensor.matmul(product[:], weights[:, block * P : (block + 1) * P], s[:], start=True, stop=True)
+                scaled = held.tile([P, PIECE], F32, name=f"scaled{piece}{block}")
+                nc.scalar.mul(scaled[:], product[:], SCALING)
+                mixed.append(scaled)
 
-        spread = psum.tile([P, SAMPLES], F32, name="spread")
-        for b in range(SAMPLES // P):
-            nc.tensor.transpose(spread[:, b * P : (b + 1) * P], inverse[:, b : b + 1].to_broadcast([P, P]), identity[:])
+            spread = psum.tile([P, PIECE], F32, name=f"spread{piece}")
+            for b in range(PIECE // P):
+                nc.tensor.transpose(spread[:, b * P : (b + 1) * P], inverse[:, b : b + 1].to_broadcast([P, P]), identity[:])
 
-        for block in range(ENTRIES // P):
-            result = held.tile([P, SAMPLES], F32, name=f"result{block}")
-            nc.vector.tensor_tensor(result[:], mixed[block][:], spread[:], MULT)
-            nc.sync.dma_start(out[block * P : (block + 1) * P, :], result[:])
+            for block in range(ENTRIES // P):
+                result = held.tile([P, PIECE], F32, name=f"result{piece}{block}")
+                nc.vector.tensor_tensor(result[:], mixed[block][:], spread[:], MULT)
+                nc.sync.dma_start(out[block * P : (block + 1) * P, piece * PIECE : (piece + 1) * PIECE], result[:])

@@ -15,6 +15,7 @@ ENTRIES = 256
 SAMPLES = 512
 PIECE = 256
 SCALING = 0.25
+WARM_UP_MATMULS = 16
 
 FLOPS = 2 * SKILLS * ENTRIES * SAMPLES
 BYTES = 4 * SKILLS * SAMPLES + 2 * SKILLS * ENTRIES + 2 * SKILLS * (SAMPLES // 16) + 4 * ENTRIES * SAMPLES
@@ -38,6 +39,12 @@ def tile_skilledloralinear_kernel(tc, skill_logits, a_w, offs, out):
         identity = held.tile([P, P], F32, name="identity")
         masks.make_identity(nc, identity[:])
 
+        zeros = held.tile([P, 512], BF16, name="zeros")
+        nc.vector.memset(zeros[:], 0.0)
+        unread = psum.tile([P, 512], F32, name="unread")
+        for repeat in range(WARM_UP_MATMULS):
+            nc.tensor.matmul(unread[:], zeros[:, :P], zeros[:], start=True, stop=True)
+
         scratch = held.tile([SKILLS, 1], F32, name="scratch")
         nc.vector.memset(scratch[:], 0.0)
         nc.scalar.activation(scratch[:], scratch[:], SIGMOID)
@@ -51,14 +58,15 @@ def tile_skilledloralinear_kernel(tc, skill_logits, a_w, offs, out):
             nc.scalar.activation(s[:], picked[:], SIGMOID)
             routing.append(s)
 
+        all_totals = psum.tile([P, SAMPLES // P], F32, name="all_totals")
         for piece in range(SAMPLES // PIECE):
             s = routing[piece]
 
-            totals = psum.tile([P, PIECE // P], F32, name=f"totals{piece}")
+            totals = all_totals[:, piece * (PIECE // P) : (piece + 1) * (PIECE // P)]
             for b in range(PIECE // P):
                 nc.tensor.matmul(totals[:, b : b + 1], s[:, b * P : (b + 1) * P], ones_column[:], start=True, stop=True)
             inverse = held.tile([P, PIECE // P], F32, name=f"inverse{piece}")
-            nc.vector.reciprocal(inverse[:], totals[:])
+            nc.vector.reciprocal(inverse[:], totals)
 
             mixed = []
             for block in range(ENTRIES // P):

@@ -30,9 +30,10 @@ def tile_skilledloralinear_kernel(tc, skill_logits, a_w, offs, out):
         offsets = held.tile([SKILLS, SAMPLES // 16], U16, name="offsets")
         nc.sync.dma_start(offsets[:], offs)
         logits = held.tile([SKILLS, TASKS], F32, name="logits")
-        nc.sync.dma_start(logits[:], skill_logits)
+        nc.sync.dma_start(logits[:, : TASKS // 2], skill_logits[:, : TASKS // 2])
+        nc.scalar.dma_start(logits[:, TASKS // 2 :], skill_logits[:, TASKS // 2 :])
         weights = held.tile([SKILLS, ENTRIES], BF16, name="weights")
-        nc.scalar.dma_start(weights[:], a_w)
+        nc.sync.dma_start(weights[:], a_w)
 
         ones_column = held.tile([SKILLS, 1], BF16, name="ones_column")
         nc.vector.memset(ones_column[:], 1.0)

@@ -15,7 +15,7 @@ ENTRIES = 256
 SAMPLES = 512
 PIECE = 256
 SCALING = 0.25
-WARM_UP_MATMULS = 16
+WARM_UP_MATMULS = 12
 
 FLOPS = 2 * SKILLS * ENTRIES * SAMPLES
 BYTES = 4 * SKILLS * SAMPLES + 2 * SKILLS * ENTRIES + 2 * SKILLS * (SAMPLES // 16) + 4 * ENTRIES * SAMPLES

@@ -84,4 +84,6 @@ def tile_skilledloralinear_kernel(tc, skill_logits, a_w, offs, out):
             for block in range(ENTRIES // P):
                 result = held.tile([P, PIECE], F32, name=f"result{piece}{block}")
                 nc.vector.tensor_tensor(result[:], mixed[block][:], spread[:], MULT)
-                nc.sync.dma_start(out[block * P : (block + 1) * P, piece * PIECE : (piece + 1) * PIECE], result[:])
+                last_piece = piece == SAMPLES // PIECE - 1
+                queue = nc.scalar if last_piece and block == 0 else nc.sync
+                queue.dma_start(out[block * P : (block + 1) * P, piece * PIECE : (piece + 1) * PIECE], result[:])

@@ -59,11 +59,12 @@ def tile_skilledloralinear_kernel(tc, skill_logits, a_w, offs, out):
             nc.scalar.activation(s[:], picked[:], SIGMOID)
             routing.append(s)
 
-        all_totals = psum.tile([P, SAMPLES // P], F32, name="all_totals")
         for piece in range(SAMPLES // PIECE):
             s = routing[piece]
 
-            totals = all_totals[:, piece * (PIECE // P) : (piece + 1) * (PIECE // P)]
+            bank = psum.tile([P, PIECE + PIECE // P], F32, name=f"bank{piece}")
+            spread = bank[:, :PIECE]
+            totals = bank[:, PIECE:]
             for b in range(PIECE // P):
                 nc.tensor.matmul(totals[:, b : b + 1], s[:, b * P : (b + 1) * P], ones_column[:], start=True, stop=True)
             inverse = held.tile([P, PIECE // P], F32, name=f"inverse{piece}")
@@ -77,13 +78,12 @@ def tile_skilledloralinear_kernel(tc, skill_logits, a_w, offs, out):
                 nc.scalar.mul(scaled[:], product[:], SCALING)
                 mixed.append(scaled)
 
-            spread = psum.tile([P, PIECE], F32, name=f"spread{piece}")
             for b in range(PIECE // P):
                 nc.tensor.transpose(spread[:, b * P : (b + 1) * P], inverse[:, b : b + 1].to_broadcast([P, P]), identity[:])
 
             for block in range(ENTRIES // P):
                 result = held.tile([P, PIECE], F32, name=f"result{piece}{block}")
-                nc.vector.tensor_tensor(result[:], mixed[block][:], spread[:], MULT)
+                nc.vector.tensor_tensor(result[:], mixed[block][:], spread, MULT)
                 last_piece = piece == SAMPLES // PIECE - 1
                 queue = nc.scalar if last_piece and block == 0 else nc.sync
                 queue.dma_start(out[block * P : (block + 1) * P, piece * PIECE : (piece + 1) * PIECE], result[:])

@@ -59,12 +59,12 @@ def tile_skilledloralinear_kernel(tc, skill_logits, a_w, offs, out):
             nc.scalar.activation(s[:], picked[:], SIGMOID)
             routing.append(s)
 
+        sums_and_product = psum.tile([P, PIECE // P + PIECE], F32, name="sums_and_product")
+        sums_and_spread = psum.tile([P, PIECE // P + PIECE], F32, name="sums_and_spread")
         for piece in range(SAMPLES // PIECE):
             s = routing[piece]
 
-            bank = psum.tile([P, PIECE + PIECE // P], F32, name=f"bank{piece}")
-            spread = bank[:, :PIECE]
-            totals = bank[:, PIECE:]
+            totals = (sums_and_product, sums_and_spread)[piece][:, : PIECE // P]
             for b in range(PIECE // P):
                 nc.tensor.matmul(totals[:, b : b + 1], s[:, b * P : (b + 1) * P], ones_column[:], start=True, stop=True)
             inverse = held.tile([P, PIECE // P], F32, name=f"inverse{piece}")
@@ -72,12 +72,19 @@ def tile_skilledloralinear_kernel(tc, skill_logits, a_w, offs, out):
 
             mixed = []
             for block in range(ENTRIES // P):
-                product = psum.tile([P, PIECE], F32, name=f"product{piece}{block}")
-                nc.tensor.matmul(product[:], weights[:, block * P : (block + 1) * P], s[:], start=True, stop=True)
+                if piece == 1 and block == 0:
+                    product = sums_and_product[:, PIECE // P :]
+                else:
+                    product = psum.tile([P, PIECE], F32, name=f"product{piece}{block}")[:]
+                nc.tensor.matmul(product, weights[:, block * P : (block + 1) * P], s[:], start=True, stop=True)
                 scaled = held.tile([P, PIECE], F32, name=f"scaled{piece}{block}")
-                nc.scalar.mul(scaled[:], product[:], SCALING)
+                nc.scalar.mul(scaled[:], product, SCALING)
                 mixed.append(scaled)
 
+            if piece == 1:
+                spread = sums_and_spread[:, PIECE // P :]
+            else:
+                spread = psum.tile([P, PIECE], F32, name=f"spread{piece}")[:]
             for b in range(PIECE // P):
                 nc.tensor.transpose(spread[:, b * P : (b + 1) * P], inverse[:, b : b + 1].to_broadcast([P, P]), identity[:])
 

@@ -78,7 +78,10 @@ def tile_skilledloralinear_kernel(tc, skill_logits, a_w, offs, out):
                     product = psum.tile([P, PIECE], F32, name=f"product{piece}{block}")[:]
                 nc.tensor.matmul(product, weights[:, block * P : (block + 1) * P], s[:], start=True, stop=True)
                 scaled = held.tile([P, PIECE], F32, name=f"scaled{piece}{block}")
-                nc.scalar.mul(scaled[:], product, SCALING)
+                if piece == 0 and block == 0:
+                    nc.vector.tensor_scalar_mul(scaled[:], product, SCALING)
+                else:
+                    nc.scalar.mul(scaled[:], product, SCALING)
                 mixed.append(scaled)
 
             if piece == 1:

@@ -27,11 +27,11 @@ def tile_skilledloralinear_kernel(tc, skill_logits, a_w, offs, out):
         tc.tile_pool(name="held", bufs=1) as held,
         tc.psum_pool(name="psum", bufs=1) as psum,
     ):
-        offsets = held.tile([SKILLS, SAMPLES // 16], U16, name="offsets")
-        nc.sync.dma_start(offsets[:], offs)
         logits = held.tile([SKILLS, TASKS], F32, name="logits")
         nc.sync.dma_start(logits[:, : TASKS // 2], skill_logits[:, : TASKS // 2])
         nc.scalar.dma_start(logits[:, TASKS // 2 :], skill_logits[:, TASKS // 2 :])
+        offsets = held.tile([SKILLS, SAMPLES // 16], U16, name="offsets")
+        nc.sync.dma_start(offsets[:], offs)
         weights = held.tile([SKILLS, ENTRIES], BF16, name="weights")
         nc.sync.dma_start(weights[:], a_w)
 

@@ -14,7 +14,7 @@ TASKS = 2048
 ENTRIES = 256
 SAMPLES = 512
 PIECE = 256
-SCALING = 0.25
+RANK = 4.0
 WARM_UP_MATMULS = 12
 
 FLOPS = 2 * SKILLS * ENTRIES * SAMPLES
@@ -35,8 +35,8 @@ def tile_skilledloralinear_kernel(tc, skill_logits, a_w, offs, out):
         weights = held.tile([SKILLS, ENTRIES], BF16, name="weights")
         nc.sync.dma_start(weights[:], a_w)
 
-        ones_column = held.tile([SKILLS, 1], BF16, name="ones_column")
-        nc.vector.memset(ones_column[:], 1.0)
+        rank_column = held.tile([SKILLS, 1], BF16, name="rank_column")
+        nc.vector.memset(rank_column[:], RANK)
         identity = held.tile([P, P], F32, name="identity")
         masks.make_identity(nc, identity[:])
 
@@ -56,7 +56,8 @@ def tile_skilledloralinear_kernel(tc, skill_logits, a_w, offs, out):
             piece_offsets = offsets[:, piece * (PIECE // 16) : (piece + 1) * (PIECE // 16)]
             nc.scalar.activation(picked[:], logits[:].indirect(piece_offsets), COPY)
             s = held.tile([SKILLS, PIECE], BF16, name=f"s{piece}")
-            nc.scalar.activation(s[:], picked[:], SIGMOID)
+            for half in range(PIECE // P):
+                nc.scalar.activation(s[:, half * P : (half + 1) * P], picked[:, half * P : (half + 1) * P], SIGMOID)
             routing.append(s)
 
         sums_and_product = psum.tile([P, PIECE // P + PIECE], F32, name="sums_and_product")
@@ -66,7 +67,7 @@ def tile_skilledloralinear_kernel(tc, skill_logits, a_w, offs, out):
 
             totals = (sums_and_product, sums_and_spread)[piece][:, : PIECE // P]
             for b in range(PIECE // P):
-                nc.tensor.matmul(totals[:, b : b + 1], s[:, b * P : (b + 1) * P], ones_column[:], start=True, stop=True)
+                nc.tensor.matmul(totals[:, b : b + 1], s[:, b * P : (b + 1) * P], rank_column[:], start=True, stop=True)
             inverse = held.tile([P, PIECE // P], F32, name=f"inverse{piece}")
             nc.vector.reciprocal(inverse[:], totals)
 
@@ -77,12 +78,12 @@ def tile_skilledloralinear_kernel(tc, skill_logits, a_w, offs, out):
                 else:
                     product = psum.tile([P, PIECE], F32, name=f"product{piece}{block}")[:]
                 nc.tensor.matmul(product, weights[:, block * P : (block + 1) * P], s[:], start=True, stop=True)
-                scaled = held.tile([P, PIECE], F32, name=f"scaled{piece}{block}")
+                unnormalised = held.tile([P, PIECE], F32, name=f"unnormalised{piece}{block}")
                 if piece == 0 and block == 0:
-                    nc.vector.tensor_scalar_mul(scaled[:], product, SCALING)
+                    nc.vector.tensor_copy(unnormalised[:], product)
                 else:
-                    nc.scalar.mul(scaled[:], product, SCALING)
-                mixed.append(scaled)
+                    nc.scalar.copy(unnormalised[:], product)
+                mixed.append(unnormalised)
 
             if piece == 1:
                 spread = sums_and_spread[:, PIECE // P :]

@@ -79,7 +79,7 @@ def tile_skilledloralinear_kernel(tc, skill_logits, a_w, offs, out):
                     product = psum.tile([P, PIECE], F32, name=f"product{piece}{block}")[:]
                 nc.tensor.matmul(product, weights[:, block * P : (block + 1) * P], s[:], start=True, stop=True)
                 unnormalised = held.tile([P, PIECE], F32, name=f"unnormalised{piece}{block}")
-                if piece == 0 and block == 0:
+                if piece == block:
                     nc.vector.tensor_copy(unnormalised[:], product)
                 else:
                     nc.scalar.copy(unnormalised[:], product)

import concourse.masks as masks
import concourse.mybir as mybir

F32 = mybir.dt.float32
BF16 = mybir.dt.bfloat16
U16 = mybir.dt.uint16
COPY = mybir.ActivationFunctionType.Copy
SIGMOID = mybir.ActivationFunctionType.Sigmoid
MULT = mybir.AluOpType.mult

P = 128
SKILLS = 128
TASKS = 2048
ENTRIES = 256
SAMPLES = 512
PIECE = 256
RANK = 4.0
WARM_UP_MATMULS = 12

FLOPS = 2 * SKILLS * ENTRIES * SAMPLES
BYTES = 4 * SKILLS * SAMPLES + 2 * SKILLS * ENTRIES + 2 * SKILLS * (SAMPLES // 16) + 4 * ENTRIES * SAMPLES


def tile_skilledloralinear_kernel(tc, skill_logits, a_w, offs, out):
    nc = tc.nc
    with (
        tc.tile_pool(name="held", bufs=1) as held,
        tc.psum_pool(name="psum", bufs=1) as psum,
    ):
        logits = held.tile([SKILLS, TASKS], F32, name="logits")
        nc.sync.dma_start(logits[:, : TASKS // 2], skill_logits[:, : TASKS // 2])
        nc.scalar.dma_start(logits[:, TASKS // 2 :], skill_logits[:, TASKS // 2 :])
        offsets = held.tile([SKILLS, SAMPLES // 16], U16, name="offsets")
        nc.sync.dma_start(offsets[:], offs)
        weights = held.tile([SKILLS, ENTRIES], BF16, name="weights")
        nc.sync.dma_start(weights[:], a_w)

        rank_column = held.tile([SKILLS, 1], BF16, name="rank_column")
        nc.vector.memset(rank_column[:], RANK)
        identity = held.tile([P, P], F32, name="identity")
        masks.make_identity(nc, identity[:])

        zeros = held.tile([P, 512], BF16, name="zeros")
        nc.vector.memset(zeros[:], 0.0)
        unread = psum.tile([P, 512], F32, name="unread")
        for repeat in range(WARM_UP_MATMULS):
            nc.tensor.matmul(unread[:], zeros[:, :P], zeros[:], start=True, stop=True)

        scratch = held.tile([SKILLS, 1], F32, name="scratch")
        nc.vector.memset(scratch[:], 0.0)
        nc.scalar.activation(scratch[:], scratch[:], SIGMOID)

        routing = []
        for piece in range(SAMPLES // PIECE):
            picked = held.tile([SKILLS, PIECE], F32, name=f"picked{piece}")
            piece_offsets = offsets[:, piece * (PIECE // 16) : (piece + 1) * (PIECE // 16)]
            nc.scalar.activation(picked[:], logits[:].indirect(piece_offsets), COPY)
            s = held.tile([SKILLS, PIECE], BF16, name=f"s{piece}")
            for half in range(PIECE // P):
                nc.scalar.activation(s[:, half * P : (half + 1) * P], picked[:, half * P : (half + 1) * P], SIGMOID)
            routing.append(s)

        sums_and_product = psum.tile([P, PIECE // P + PIECE], F32, name="sums_and_product")
        sums_and_spread = psum.tile([P, PIECE // P + PIECE], F32, name="sums_and_spread")
        for piece in range(SAMPLES // PIECE):
            s = routing[piece]

            totals = (sums_and_product, sums_and_spread)[piece][:, : PIECE // P]
            for b in range(PIECE // P):
                nc.tensor.matmul(totals[:, b : b + 1], s[:, b * P : (b + 1) * P], rank_column[:], start=True, stop=True)
            inverse = held.tile([P, PIECE // P], F32, name=f"inverse{piece}")
            nc.vector.reciprocal(inverse[:], totals)

            mixed = []
            for block in range(ENTRIES // P):
                if piece == 1 and block == 0:
                    product = sums_and_product[:, PIECE // P :]
                else:
                    product = psum.tile([P, PIECE], F32, name=f"product{piece}{block}")[:]
                nc.tensor.matmul(product, weights[:, block * P : (block + 1) * P], s[:], start=True, stop=True)
                unnormalised = held.tile([P, PIECE], F32, name=f"unnormalised{piece}{block}")
                if piece == block:
                    nc.vector.tensor_copy(unnormalised[:], product)
                else:
                    nc.scalar.copy(unnormalised[:], product)
                mixed.append(unnormalised)

            if piece == 1:
                spread = sums_and_spread[:, PIECE // P :]
            else:
                spread = psum.tile([P, PIECE], F32, name=f"spread{piece}")[:]
            for b in range(PIECE // P):
                nc.tensor.transpose(spread[:, b * P : (b + 1) * P], inverse[:, b : b + 1].to_broadcast([P, P]), identity[:])

            for block in range(ENTRIES // P):
                result = held.tile([P, PIECE], F32, name=f"result{piece}{block}")
                nc.vector.tensor_tensor(result[:], mixed[block][:], spread, MULT)
                last_piece = piece == SAMPLES // PIECE - 1
                queue = nc.scalar if last_piece and block == 0 else nc.sync
                queue.dma_start(out[block * P : (block + 1) * P, piece * PIECE : (piece + 1) * PIECE], result[:])
